import numpy as np
import ml_dtypes


def mxq(x, axis, fmt="e4m3"):
    dtype, down = {"e4m3": (ml_dtypes.float8_e4m3fn, 7), "e5m2": (ml_dtypes.float8_e5m2, 14)}[fmt]
    v = np.moveaxis(np.asarray(x, np.float32).astype(ml_dtypes.bfloat16).astype(np.float64), axis, -1)
    blocks = v.reshape(v.shape[:-1] + (-1, 32))
    amax = np.abs(blocks).max(-1, keepdims=True)
    byte = np.maximum(np.where(amax > 0, np.frexp(amax)[1] - 1 + 127, 0) - down, 1)
    scale = np.exp2(byte - 127.0)
    codes = (blocks / scale).astype(np.float32).astype(dtype).astype(np.float64)
    return np.moveaxis((codes * scale).reshape(v.shape), -1, axis)


WIDE = False


def mx_kscale(k):
    if not WIDE:
        return np.ones(k)
    levels = np.array([20, -20, 10, -10, 0])
    a = np.random.permutation(np.resize(levels, k // 512 * 4)).reshape(k // 512, 4)
    idx = np.arange(k)
    return np.exp2(a[idx // 512, idx % 128 // 32])


BF16 = ml_dtypes.bfloat16


def bf(x):
    return np.asarray(x, np.float32).astype(BF16)


def f64(x):
    return np.asarray(x).astype(np.float64)


BS, CIN, COUT, OUT_DIM, BLK = 512, 128, 512, 8, 4
D = OUT_DIM * BLK


def setup_inputs():
    s = mx_kscale(BS)[:, None, None]
    x = np.random.standard_normal((BS, CIN, D)) * s
    weight = np.random.standard_normal((COUT, CIN, D))
    g = np.random.standard_normal((BS, COUT, OUT_DIM)) * np.exp2(np.random.randint(-12, 1, (BS, 1, OUT_DIM))) * 4.0 / s
    return {"x": bf(x), "weight": bf(weight), "grad_out": bf(g)}


def reference(x, weight, grad_out):
    bs, cin, d = x.shape
    cout = weight.shape[0]
    n = d // BLK
    xr = f64(x).reshape(bs, cin, n, BLK).transpose(2, 0, 1, 3).reshape(n, bs, cin * BLK)
    gr = f64(grad_out).transpose(2, 0, 1)
    gw = mxq(gr, 1, "e5m2").transpose(0, 2, 1) @ mxq(xr, 1, "e4m3")
    gw = gw.reshape(n, cout, cin, BLK).transpose(1, 2, 0, 3).reshape(cout, cin, d)
    return gw / np.sqrt(cin)

@@ -1,0 +1,148 @@
+import math
+from contextlib import ExitStack
+
+import concourse.mybir as mybir
+
+FLOPS = 2 * 8 * 512 * 512 * 512
+BYTES = 2 * 512 * 128 * 32 + 2 * 512 * 512 * 8 + 4 * 512 * 128 * 32
+
+BF16 = mybir.dt.bfloat16
+F32 = mybir.dt.float32
+U32 = mybir.dt.uint32
+U8 = mybir.dt.uint8
+E4M3X4 = mybir.dt.float8_e4m3fn_x4
+E5M2X4 = mybir.dt.float8_e5m2_x4
+
+P = 128
+PACK = 4
+CIN = 128
+COUT = 512
+NPOS = 8
+BLK = 4
+X_CHUNKS = (32, 32, 32, 32)
+X_VECTOR_POSITIONS = 4
+PINNED = True
+
+
+def tile_nonoverlappinglocallyconnected1d_kernel(tc, x, weight, grad_out, out):
+    nc = tc.nc
+    inv = 1.0 / math.sqrt(float(CIN))
+    xv = x.rearrange("(p j) i d -> p j (i d)", j=PACK)
+    gv = grad_out.rearrange("(p j) o n -> p j (o n)", j=PACK)
+    ov = out.rearrange("(t o) i d -> t o (i d)", o=P)
+    n_tiles = COUT // P
+
+    with ExitStack() as ctx:
+        raw = ctx.enter_context(tc.tile_pool(name="raw", bufs=1))
+        grp = ctx.enter_context(tc.tile_pool(name="grp", bufs=4))
+        keep = ctx.enter_context(tc.tile_pool(name="keep", bufs=1))
+        res = ctx.enter_context(tc.tile_pool(name="res", bufs=6))
+        psum = ctx.enter_context(tc.psum_pool(name="psum", bufs=8))
+        if PINNED:
+            ctx.enter_context(tc.manual_schedule())
+
+        xq = keep.tile([P, NPOS, CIN * BLK], U32, name="xq", align_bytes=64)
+        xs = keep.tile([P, NPOS, CIN * BLK], U8, name="xs", align_bytes=64)
+        gq = keep.tile([P, n_tiles, NPOS * P], U32, name="gq", align_bytes=64)
+        gs = keep.tile([P, n_tiles, NPOS * P], U8, name="gs", align_bytes=64)
+
+        xr = []
+        i0s = []
+        i0 = 0
+        for c, ic in enumerate(X_CHUNKS):
+            t_ = raw.tile([P, PACK, ic * 32], BF16, name="xr%d" % c)
+            nc.sync.dma_start(out=t_[:], in_=xv[:, :, i0 * 32 : (i0 + ic) * 32])
+            xr.append(t_)
+            i0s.append(i0)
+            i0 += ic
+        gr = []
+        for t in range(n_tiles):
+            t_ = raw.tile([P, PACK, P * NPOS], BF16, name="gr%d" % t)
+            nc.sync.dma_start(out=t_[:], in_=gv[:, :, t * P * NPOS : (t + 1) * P * NPOS])
+            gr.append(t_)
+
+        xg = {}
+        gg = {}
+
+        def copy_x(c):
+            ic = X_CHUNKS[c]
+            dst = grp.tile([P, NPOS, ic * 16], BF16, name="xg%d" % c, tag="grp", align_bytes=64)
+            xg[c] = dst
+            nv = X_VECTOR_POSITIONS
+            nc.vector.tensor_copy(
+                out=dst[:].rearrange("p n (i k j) -> p i n j k", k=BLK, j=PACK)[:, :, 0:nv],
+                in_=xr[c][:].rearrange("p j (i n k) -> p i n j k", n=NPOS, k=BLK)[:, :, 0:nv],
+            )
+            for n in range(nv, NPOS):
+                nc.scalar.copy(
+                    out=dst[:, n, :].rearrange("p (i k j) -> p i j k", k=BLK, j=PACK),
+                    in_=xr[c][:].rearrange("p j (i n k) -> p n i j k", n=NPOS, k=BLK)[:, n],
+                )
+
+        def quant_x(c):
+            ic = X_CHUNKS[c]
+            w0 = i0s[c] * BLK
+            w1 = w0 + ic * BLK
+            for n in range(NPOS):
+                nc.vector.quantize_mx(
+                    out=xq[:, n, w0:w1].bitcast(E4M3X4),
+                    scales=xs[:, n, w0:w1],
+                    in_=xg[c][:, n, :],
+                )
+
+        def copy_g(t, h):
+            if h == 0:
+                gg[t] = grp.tile([P, NPOS, P * PACK], BF16, name="gg%d" % t, tag="grp", align_bytes=64)
+            nc.vector.tensor_copy(
+                out=gg[t][:].rearrange("p (h l) (o j) -> p h o j l", l=4, j=PACK)[:, h],
+                in_=gr[t][:].rearrange("p j (o h l) -> p h o j l", h=2, l=4)[:, h],
+            )
+
+        def quant_g(t, h):
+            nc.vector.quantize_mx(
+                out=gq[:, t, h * 512 : (h + 1) * 512].bitcast(E5M2X4),
+                scales=gs[:, t, h * 512 : (h + 1) * 512],
+                in_=gg[t][:, 4 * h : 4 * h + 4, :].rearrange("p n c -> p (n c)"),
+            )
+
+        def finish(t):
+            banks = []
+            for n in range(NPOS):
+                ps = psum.tile([P, CIN * BLK], F32, name="ps%d_%d" % (t, n), tag="ps")
+                nc.tensor.matmul_mx(
+                    out=ps[:],
+                    lhsT=gq[:, t, n * P : (n + 1) * P].bitcast(E5M2X4),
+                    lhsT_scale=gs[:, t, n * P : (n + 1) * P],
+                    rhs=xq[:, n, :].bitcast(E4M3X4),
+                    rhs_scale=xs[:, n, :],
+                    start=True,
+                    stop=True,
+                )
+                banks.append(ps)
+            for h in range(2):
+                ob = res.tile([P, 64 * 32], F32, name="ob%d_%d" % (t, h), tag="ob")
+                for n in range(NPOS):
+                    nc.scalar.mul(
+                        out=ob[:].rearrange("p (i n k) -> p i n k", n=NPOS, k=BLK)[:, :, n, :],
+                        in_=banks[n][:, h * 256 : (h + 1) * 256].rearrange("p (i k) -> p i k", k=BLK),
+                        mul=inv,
+                    )
+                nc.sync.dma_start(out=ov[t][:, h * 2048 : (h + 1) * 2048], in_=ob[:])
+
+        nx = len(X_CHUNKS)
+        copy_x(0)
+        for c in range(1, nx):
+            copy_x(c)
+            quant_x(c - 1)
+        copy_g(0, 0)
+        quant_x(nx - 1)
+        copy_g(0, 1)
+        quant_g(0, 0)
+        for t in range(n_tiles):
+            if t + 1 < n_tiles:
+                copy_g(t + 1, 0)
+            quant_g(t, 1)
+            finish(t)
+            if t + 1 < n_tiles:
+                copy_g(t + 1, 1)
+                quant_g(t + 1, 0)

@@ -19,9 +19,17 @@ CIN = 128
 COUT = 512
 NPOS = 8
 BLK = 4
-X_CHUNKS = (32, 32, 32, 32)
-X_VECTOR_POSITIONS = 4
-PINNED = True
+IC = 32
+NX = CIN // IC
+NV = 3
+
+
+def vector_share(t, h):
+    if t == 0:
+        return ()
+    if t < 3:
+        return (6, 7) if h == 1 else ()
+    return (4, 5, 6, 7)
 
 
 def tile_nonoverlappinglocallyconnected1d_kernel(tc, x, weight, grad_out, out):
@@ -31,6 +39,7 @@ def tile_nonoverlappinglocallyconnected1d_kernel(tc, x, weight, grad_out, out):
     gv = grad_out.rearrange("(p j) o n -> p j (o n)", j=PACK)
     ov = out.rearrange("(t o) i d -> t o (i d)", o=P)
     n_tiles = COUT // P
+    gw = P * NPOS
 
     with ExitStack() as ctx:
         raw = ctx.enter_context(tc.tile_pool(name="raw", bufs=1))
@@ -38,64 +47,65 @@ def tile_nonoverlappinglocallyconnected1d_kernel(tc, x, weight, grad_out, out):
         keep = ctx.enter_context(tc.tile_pool(name="keep", bufs=1))
         res = ctx.enter_context(tc.tile_pool(name="res", bufs=6))
         psum = ctx.enter_context(tc.psum_pool(name="psum", bufs=8))
-        if PINNED:
-            ctx.enter_context(tc.manual_schedule())
+        ctx.enter_context(tc.manual_schedule())
 
         xq = keep.tile([P, NPOS, CIN * BLK], U32, name="xq", align_bytes=64)
         xs = keep.tile([P, NPOS, CIN * BLK], U8, name="xs", align_bytes=64)
-        gq = keep.tile([P, n_tiles, NPOS * P], U32, name="gq", align_bytes=64)
-        gs = keep.tile([P, n_tiles, NPOS * P], U8, name="gs", align_bytes=64)
+        gq = keep.tile([P, n_tiles, gw], U32, name="gq", align_bytes=64)
+        gs = keep.tile([P, n_tiles, gw], U8, name="gs", align_bytes=64)
 
-        xr = []
-        i0s = []
-        i0 = 0
-        for c, ic in enumerate(X_CHUNKS):
-            t_ = raw.tile([P, PACK, ic * 32], BF16, name="xr%d" % c)
-            nc.sync.dma_start(out=t_[:], in_=xv[:, :, i0 * 32 : (i0 + ic) * 32])
-            xr.append(t_)
-            i0s.append(i0)
-            i0 += ic
-        gr = []
-        for t in range(n_tiles):
-            t_ = raw.tile([P, PACK, P * NPOS], BF16, name="gr%d" % t)
-            nc.sync.dma_start(out=t_[:], in_=gv[:, :, t * P * NPOS : (t + 1) * P * NPOS])
-            gr.append(t_)
+        xr = {}
+        gr = {}
+
+        def load_x(c):
+            xr[c] = raw.tile([P, PACK, IC * 32], BF16, name="xr%d" % c)
+            nc.sync.dma_start(out=xr[c][:], in_=xv[:, :, c * IC * 32 : (c + 1) * IC * 32])
+
+        def load_g(t0, t1):
+            buf = raw.tile([P, PACK, (t1 - t0) * gw], BF16, name="gr%d" % t0)
+            nc.sync.dma_start(out=buf[:], in_=gv[:, :, t0 * gw : t1 * gw])
+            for t in range(t0, t1):
+                gr[t] = buf[:, :, (t - t0) * gw : (t - t0 + 1) * gw]
+
+        load_x(0)
+        load_x(1)
+        load_g(0, 1)
+        load_x(2)
+        load_x(3)
+        load_g(1, 2)
+        load_g(2, 4)
 
         xg = {}
         gg = {}
 
         def copy_x(c):
-            ic = X_CHUNKS[c]
-            dst = grp.tile([P, NPOS, ic * 16], BF16, name="xg%d" % c, tag="grp", align_bytes=64)
+            dst = grp.tile([P, NPOS, IC * 16], BF16, name="xg%d" % c, tag="grp", align_bytes=64)
             xg[c] = dst
-            nv = X_VECTOR_POSITIONS
             nc.vector.tensor_copy(
-                out=dst[:].rearrange("p n (i k j) -> p i n j k", k=BLK, j=PACK)[:, :, 0:nv],
-                in_=xr[c][:].rearrange("p j (i n k) -> p i n j k", n=NPOS, k=BLK)[:, :, 0:nv],
+                out=dst[:].rearrange("p n (i k j) -> p i n j k", k=BLK, j=PACK)[:, :, 0:NV],
+                in_=xr[c][:].rearrange("p j (i n k) -> p i n j k", n=NPOS, k=BLK)[:, :, 0:NV],
             )
-            for n in range(nv, NPOS):
+            for n in range(NV, NPOS):
                 nc.scalar.copy(
                     out=dst[:, n, :].rearrange("p (i k j) -> p i j k", k=BLK, j=PACK),
                     in_=xr[c][:].rearrange("p j (i n k) -> p n i j k", n=NPOS, k=BLK)[:, n],
                 )
 
-        def quant_x(c):
-            ic = X_CHUNKS[c]
-            w0 = i0s[c] * BLK
-            w1 = w0 + ic * BLK
-            for n in range(NPOS):
-                nc.vector.quantize_mx(
-                    out=xq[:, n, w0:w1].bitcast(E4M3X4),
-                    scales=xs[:, n, w0:w1],
-                    in_=xg[c][:, n, :],
-                )
+        def quant_x(c, n):
+            w0 = c * IC * BLK
+            w1 = w0 + IC * BLK
+            nc.vector.quantize_mx(
+                out=xq[:, n, w0:w1].bitcast(E4M3X4),
+                scales=xs[:, n, w0:w1],
+                in_=xg[c][:, n, :],
+            )
 
         def copy_g(t, h):
             if h == 0:
                 gg[t] = grp.tile([P, NPOS, P * PACK], BF16, name="gg%d" % t, tag="grp", align_bytes=64)
             nc.vector.tensor_copy(
                 out=gg[t][:].rearrange("p (h l) (o j) -> p h o j l", l=4, j=PACK)[:, h],
-                in_=gr[t][:].rearrange("p j (o h l) -> p h o j l", h=2, l=4)[:, h],
+                in_=gr[t].rearrange("p j (o h l) -> p h o j l", h=2, l=4)[:, h],
             )
 
         def quant_g(t, h):
@@ -105,7 +115,13 @@ def tile_nonoverlappinglocallyconnected1d_kernel(tc, x, weight, grad_out, out):
                 in_=gg[t][:, 4 * h : 4 * h + 4, :].rearrange("p n c -> p (n c)"),
             )
 
-        def finish(t):
+        def prepare_g(t):
+            copy_g(t, 0)
+            copy_g(t, 1)
+            quant_g(t, 0)
+            quant_g(t, 1)
+
+        def multiply(t):
             banks = []
             for n in range(NPOS):
                 ps = psum.tile([P, CIN * BLK], F32, name="ps%d_%d" % (t, n), tag="ps")
@@ -119,30 +135,44 @@ def tile_nonoverlappinglocallyconnected1d_kernel(tc, x, weight, grad_out, out):
                     stop=True,
                 )
                 banks.append(ps)
-            for h in range(2):
-                ob = res.tile([P, 64 * 32], F32, name="ob%d_%d" % (t, h), tag="ob")
-                for n in range(NPOS):
+            return banks
+
+        def copy_out(t, h, banks):
+            ob = res.tile([P, 64 * 32], F32, name="ob%d_%d" % (t, h), tag="ob")
+            share = vector_share(t, h)
+            for n in range(NPOS):
+                if n not in share:
                     nc.scalar.mul(
                         out=ob[:].rearrange("p (i n k) -> p i n k", n=NPOS, k=BLK)[:, :, n, :],
                         in_=banks[n][:, h * 256 : (h + 1) * 256].rearrange("p (i k) -> p i k", k=BLK),
                         mul=inv,
                     )
-                nc.sync.dma_start(out=ov[t][:, h * 2048 : (h + 1) * 2048], in_=ob[:])
+            for n in share:
+                nc.vector.tensor_scalar_mul(
+                    out=ob[:].rearrange("p (i n k) -> p i n k", n=NPOS, k=BLK)[:, :, n, :],
+                    in0=banks[n][:, h * 256 : (h + 1) * 256].rearrange("p (i k) -> p i k", k=BLK),
+                    scalar1=inv,
+                )
+            nc.sync.dma_start(out=ov[t][:, h * 2048 : (h + 1) * 2048], in_=ob[:])
 
-        nx = len(X_CHUNKS)
         copy_x(0)
-        for c in range(1, nx):
-            copy_x(c)
-            quant_x(c - 1)
+        copy_x(1)
+        for n in range(NPOS):
+            quant_x(0, n)
         copy_g(0, 0)
-        quant_x(nx - 1)
         copy_g(0, 1)
+        for n in range(NPOS):
+            quant_x(1, n)
+        copy_x(2)
         quant_g(0, 0)
+        quant_g(0, 1)
+        copy_x(3)
+        for n in range(NPOS):
+            quant_x(2, n)
+            quant_x(3, n)
         for t in range(n_tiles):
+            banks = multiply(t)
+            copy_out(t, 0, banks)
             if t + 1 < n_tiles:
-                copy_g(t + 1, 0)
-            quant_g(t, 1)
-            finish(t)
-            if t + 1 < n_tiles:
-                copy_g(t + 1, 1)
-                quant_g(t + 1, 0)
+                prepare_g(t + 1)
+            copy_out(t, 1, banks)

@@ -47,7 +47,6 @@ def tile_nonoverlappinglocallyconnected1d_kernel(tc, x, weight, grad_out, out):
         keep = ctx.enter_context(tc.tile_pool(name="keep", bufs=1))
         res = ctx.enter_context(tc.tile_pool(name="res", bufs=6))
         psum = ctx.enter_context(tc.psum_pool(name="psum", bufs=8))
-        ctx.enter_context(tc.manual_schedule())
 
         xq = keep.tile([P, NPOS, CIN * BLK], U32, name="xq", align_bytes=64)
         xs = keep.tile([P, NPOS, CIN * BLK], U8, name="xs", align_bytes=64)

@@ -19,17 +19,11 @@ CIN = 128
 COUT = 512
 NPOS = 8
 BLK = 4
-IC = 32
-NX = CIN // IC
-NV = 3
-
-
-def vector_share(t, h):
-    if t == 0:
-        return ()
-    if t < 3:
-        return (6, 7) if h == 1 else ()
-    return (4, 5, 6, 7)
+XCH = (32, 32, 32, 32,)
+NV = (5, 3, 3, 4,)
+VPAIRS = (0, 1, 0, 1, 0, 1, 2, 2,)
+LOADS = ("x0", "x1", "g0", "x2", "x3", "g1", "g23",)
+G0H1_SCALAR = True
 
 
 def tile_nonoverlappinglocallyconnected1d_kernel(tc, x, weight, grad_out, out):
@@ -40,6 +34,8 @@ def tile_nonoverlappinglocallyconnected1d_kernel(tc, x, weight, grad_out, out):
     ov = out.rearrange("(t o) i d -> t o (i d)", o=P)
     n_tiles = COUT // P
     gw = P * NPOS
+    nx = len(XCH)
+    i0s = [sum(XCH[:c]) for c in range(nx)]
 
     with ExitStack() as ctx:
         raw = ctx.enter_context(tc.tile_pool(name="raw", bufs=1))
@@ -57,8 +53,8 @@ def tile_nonoverlappinglocallyconnected1d_kernel(tc, x, weight, grad_out, out):
         gr = {}
 
         def load_x(c):
-            xr[c] = raw.tile([P, PACK, IC * 32], BF16, name="xr%d" % c)
-            nc.sync.dma_start(out=xr[c][:], in_=xv[:, :, c * IC * 32 : (c + 1) * IC * 32])
+            xr[c] = raw.tile([P, PACK, XCH[c] * 32], BF16, name="xr%d" % c)
+            nc.sync.dma_start(out=xr[c][:], in_=xv[:, :, i0s[c] * 32 : (i0s[c] + XCH[c]) * 32])
 
         def load_g(t0, t1):
             buf = raw.tile([P, PACK, (t1 - t0) * gw], BF16, name="gr%d" % t0)
@@ -66,33 +62,34 @@ def tile_nonoverlappinglocallyconnected1d_kernel(tc, x, weight, grad_out, out):
             for t in range(t0, t1):
                 gr[t] = buf[:, :, (t - t0) * gw : (t - t0 + 1) * gw]
 
-        load_x(0)
-        load_x(1)
-        load_g(0, 1)
-        load_x(2)
-        load_x(3)
-        load_g(1, 2)
-        load_g(2, 4)
+        for item in LOADS:
+            if item[0] == "x":
+                load_x(int(item[1:]))
+            else:
+                load_g(int(item[1]), int(item[-1]) + 1)
 
         xg = {}
         gg = {}
 
         def copy_x(c):
-            dst = grp.tile([P, NPOS, IC * 16], BF16, name="xg%d" % c, tag="grp", align_bytes=64)
+            ic = XCH[c]
+            nv = NV[c]
+            dst = grp.tile([P, NPOS, ic * 16], BF16, name="xg%d" % c, tag="grp", align_bytes=64)
             xg[c] = dst
-            nc.vector.tensor_copy(
-                out=dst[:].rearrange("p n (i k j) -> p i n j k", k=BLK, j=PACK)[:, :, 0:NV],
-                in_=xr[c][:].rearrange("p j (i n k) -> p i n j k", n=NPOS, k=BLK)[:, :, 0:NV],
-            )
-            for n in range(NV, NPOS):
+            if nv > 0:
+                nc.vector.tensor_copy(
+                    out=dst[:].rearrange("p n (i k j) -> p i n j k", k=BLK, j=PACK)[:, :, 0:nv],
+                    in_=xr[c][:].rearrange("p j (i n k) -> p i n j k", n=NPOS, k=BLK)[:, :, 0:nv],
+                )
+            for n in range(nv, NPOS):
                 nc.scalar.copy(
                     out=dst[:, n, :].rearrange("p (i k j) -> p i j k", k=BLK, j=PACK),
                     in_=xr[c][:].rearrange("p j (i n k) -> p n i j k", n=NPOS, k=BLK)[:, n],
                 )
 
         def quant_x(c, n):
-            w0 = c * IC * BLK
-            w1 = w0 + IC * BLK
+            w0 = i0s[c] * BLK
+            w1 = w0 + XCH[c] * BLK
             nc.vector.quantize_mx(
                 out=xq[:, n, w0:w1].bitcast(E4M3X4),
                 scales=xs[:, n, w0:w1],
@@ -102,10 +99,12 @@ def tile_nonoverlappinglocallyconnected1d_kernel(tc, x, weight, grad_out, out):
         def copy_g(t, h):
             if h == 0:
                 gg[t] = grp.tile([P, NPOS, P * PACK], BF16, name="gg%d" % t, tag="grp", align_bytes=64)
-            nc.vector.tensor_copy(
-                out=gg[t][:].rearrange("p (h l) (o j) -> p h o j l", l=4, j=PACK)[:, h],
-                in_=gr[t].rearrange("p j (o h l) -> p h o j l", h=2, l=4)[:, h],
-            )
+            dst = gg[t][:].rearrange("p (h l) (o j) -> p h o j l", l=4, j=PACK)[:, h]
+            src = gr[t].rearrange("p j (o h l) -> p h o j l", h=2, l=4)[:, h]
+            if G0H1_SCALAR and t == 0 and h == 1:
+                nc.scalar.copy(out=dst, in_=src)
+            else:
+                nc.vector.tensor_copy(out=dst, in_=src)
 
         def quant_g(t, h):
             nc.vector.quantize_mx(
@@ -138,20 +137,14 @@ def tile_nonoverlappinglocallyconnected1d_kernel(tc, x, weight, grad_out, out):
 
         def copy_out(t, h, banks):
             ob = res.tile([P, 64 * 32], F32, name="ob%d_%d" % (t, h), tag="ob")
-            share = vector_share(t, h)
+            first_v = NPOS - 2 * VPAIRS[2 * t + h]
             for n in range(NPOS):
-                if n not in share:
-                    nc.scalar.mul(
-                        out=ob[:].rearrange("p (i n k) -> p i n k", n=NPOS, k=BLK)[:, :, n, :],
-                        in_=banks[n][:, h * 256 : (h + 1) * 256].rearrange("p (i k) -> p i k", k=BLK),
-                        mul=inv,
-                    )
-            for n in share:
-                nc.vector.tensor_scalar_mul(
-                    out=ob[:].rearrange("p (i n k) -> p i n k", n=NPOS, k=BLK)[:, :, n, :],
-                    in0=banks[n][:, h * 256 : (h + 1) * 256].rearrange("p (i k) -> p i k", k=BLK),
-                    scalar1=inv,
-                )
+                dst = ob[:].rearrange("p (i n k) -> p i n k", n=NPOS, k=BLK)[:, :, n, :]
+                src = banks[n][:, h * 256 : (h + 1) * 256].rearrange("p (i k) -> p i k", k=BLK)
+                if n < first_v:
+                    nc.scalar.mul(out=dst, in_=src, mul=inv)
+                else:
+                    nc.vector.tensor_scalar_mul(out=dst, in0=src, scalar1=inv)
             nc.sync.dma_start(out=ov[t][:, h * 2048 : (h + 1) * 2048], in_=ob[:])
 
         copy_x(0)

@@ -43,6 +43,7 @@ def tile_nonoverlappinglocallyconnected1d_kernel(tc, x, weight, grad_out, out):
         keep = ctx.enter_context(tc.tile_pool(name="keep", bufs=1))
         res = ctx.enter_context(tc.tile_pool(name="res", bufs=6))
         psum = ctx.enter_context(tc.psum_pool(name="psum", bufs=8))
+        ctx.enter_context(tc.manual_schedule())
 
         xq = keep.tile([P, NPOS, CIN * BLK], U32, name="xq", align_bytes=64)
         xs = keep.tile([P, NPOS, CIN * BLK], U8, name="xs", align_bytes=64)

@@ -19,11 +19,10 @@ CIN = 128
 COUT = 512
 NPOS = 8
 BLK = 4
-XCH = (32, 32, 32, 32,)
-NV = (5, 3, 3, 4,)
-VPAIRS = (0, 1, 0, 1, 0, 1, 2, 2,)
-LOADS = ("x0", "x1", "g0", "x2", "x3", "g1", "g23",)
-G0H1_SCALAR = True
+XC = 32
+HALF = CIN * BLK // 2
+NV = (4, 4, 6, 6)
+LOADS = ("x0", "x1", "g0", "g1", "x2", "x3", "g23")
 
 
 def tile_nonoverlappinglocallyconnected1d_kernel(tc, x, weight, grad_out, out):
@@ -34,12 +33,10 @@ def tile_nonoverlappinglocallyconnected1d_kernel(tc, x, weight, grad_out, out):
     ov = out.rearrange("(t o) i d -> t o (i d)", o=P)
     n_tiles = COUT // P
     gw = P * NPOS
-    nx = len(XCH)
-    i0s = [sum(XCH[:c]) for c in range(nx)]
 
     with ExitStack() as ctx:
         raw = ctx.enter_context(tc.tile_pool(name="raw", bufs=1))
-        grp = ctx.enter_context(tc.tile_pool(name="grp", bufs=4))
+        grp = ctx.enter_context(tc.tile_pool(name="grp", bufs=8))
         keep = ctx.enter_context(tc.tile_pool(name="keep", bufs=1))
         res = ctx.enter_context(tc.tile_pool(name="res", bufs=6))
         psum = ctx.enter_context(tc.psum_pool(name="psum", bufs=8))
@@ -54,8 +51,8 @@ def tile_nonoverlappinglocallyconnected1d_kernel(tc, x, weight, grad_out, out):
         gr = {}
 
         def load_x(c):
-            xr[c] = raw.tile([P, PACK, XCH[c] * 32], BF16, name="xr%d" % c)
-            nc.sync.dma_start(out=xr[c][:], in_=xv[:, :, i0s[c] * 32 : (i0s[c] + XCH[c]) * 32])
+            xr[c] = raw.tile([P, PACK, XC * 32], BF16, name="xr%d" % c)
+            nc.sync.dma_start(out=xr[c][:], in_=xv[:, :, c * XC * 32 : (c + 1) * XC * 32])
 
         def load_g(t0, t1):
             buf = raw.tile([P, PACK, (t1 - t0) * gw], BF16, name="gr%d" % t0)
@@ -69,19 +66,20 @@ def tile_nonoverlappinglocallyconnected1d_kernel(tc, x, weight, grad_out, out):
             else:
                 load_g(int(item[1]), int(item[-1]) + 1)
 
+        nc.vector.memset(xq[:, :, HALF:], 0)
+        nc.vector.memset(xs[:].bitcast(U32)[:, :, HALF // 4 :], 0)
+
         xg = {}
         gg = {}
 
         def copy_x(c):
-            ic = XCH[c]
             nv = NV[c]
-            dst = grp.tile([P, NPOS, ic * 16], BF16, name="xg%d" % c, tag="grp", align_bytes=64)
+            dst = grp.tile([P, NPOS, XC * 16], BF16, name="xg%d" % c, tag="grp", align_bytes=64)
             xg[c] = dst
-            if nv > 0:
-                nc.vector.tensor_copy(
-                    out=dst[:].rearrange("p n (i k j) -> p i n j k", k=BLK, j=PACK)[:, :, 0:nv],
-                    in_=xr[c][:].rearrange("p j (i n k) -> p i n j k", n=NPOS, k=BLK)[:, :, 0:nv],
-                )
+            nc.vector.tensor_copy(
+                out=dst[:].rearrange("p n (i k j) -> p i n j k", k=BLK, j=PACK)[:, :, 0:nv],
+                in_=xr[c][:].rearrange("p j (i n k) -> p i n j k", n=NPOS, k=BLK)[:, :, 0:nv],
+            )
             for n in range(nv, NPOS):
                 nc.scalar.copy(
                     out=dst[:, n, :].rearrange("p (i k j) -> p i j k", k=BLK, j=PACK),
@@ -89,20 +87,20 @@ def tile_nonoverlappinglocallyconnected1d_kernel(tc, x, weight, grad_out, out):
                 )
 
         def quant_x(c, n):
-            w0 = i0s[c] * BLK
-            w1 = w0 + XCH[c] * BLK
+            w0 = c * XC * BLK
+            w1 = w0 + XC * BLK
             nc.vector.quantize_mx(
                 out=xq[:, n, w0:w1].bitcast(E4M3X4),
                 scales=xs[:, n, w0:w1],
                 in_=xg[c][:, n, :],
             )
 
-        def copy_g(t, h):
+        def copy_g(t, h, engine):
             if h == 0:
                 gg[t] = grp.tile([P, NPOS, P * PACK], BF16, name="gg%d" % t, tag="grp", align_bytes=64)
             dst = gg[t][:].rearrange("p (h l) (o j) -> p h o j l", l=4, j=PACK)[:, h]
             src = gr[t].rearrange("p j (o h l) -> p h o j l", h=2, l=4)[:, h]
-            if G0H1_SCALAR and t == 0 and h == 1:
+            if engine == "S":
                 nc.scalar.copy(out=dst, in_=src)
             else:
                 nc.vector.tensor_copy(out=dst, in_=src)
@@ -114,58 +112,68 @@ def tile_nonoverlappinglocallyconnected1d_kernel(tc, x, weight, grad_out, out):
                 in_=gg[t][:, 4 * h : 4 * h + 4, :].rearrange("p n c -> p (n c)"),
             )
 
-        def prepare_g(t):
-            copy_g(t, 0)
-            copy_g(t, 1)
-            quant_g(t, 0)
-            quant_g(t, 1)
+        def multiply(t, n, tag):
+            ps = psum.tile([P, CIN * BLK], F32, name="ps%s%d_%d" % (tag, t, n), tag="ps")
+            nc.tensor.matmul_mx(
+                out=ps[:],
+                lhsT=gq[:, t, n * P : (n + 1) * P].bitcast(E5M2X4),
+                lhsT_scale=gs[:, t, n * P : (n + 1) * P],
+                rhs=xq[:, n, :].bitcast(E4M3X4),
+                rhs_scale=xs[:, n, :],
+                start=True,
+                stop=True,
+            )
+            return ps
 
-        def multiply(t):
-            banks = []
-            for n in range(NPOS):
-                ps = psum.tile([P, CIN * BLK], F32, name="ps%d_%d" % (t, n), tag="ps")
-                nc.tensor.matmul_mx(
-                    out=ps[:],
-                    lhsT=gq[:, t, n * P : (n + 1) * P].bitcast(E5M2X4),
-                    lhsT_scale=gs[:, t, n * P : (n + 1) * P],
-                    rhs=xq[:, n, :].bitcast(E4M3X4),
-                    rhs_scale=xs[:, n, :],
-                    start=True,
-                    stop=True,
-                )
-                banks.append(ps)
-            return banks
-
-        def copy_out(t, h, banks):
+        def copy_out(t, h, banks, nvec=0):
             ob = res.tile([P, 64 * 32], F32, name="ob%d_%d" % (t, h), tag="ob")
-            first_v = NPOS - 2 * VPAIRS[2 * t + h]
             for n in range(NPOS):
                 dst = ob[:].rearrange("p (i n k) -> p i n k", n=NPOS, k=BLK)[:, :, n, :]
                 src = banks[n][:, h * 256 : (h + 1) * 256].rearrange("p (i k) -> p i k", k=BLK)
-                if n < first_v:
+                if n < NPOS - nvec:
                     nc.scalar.mul(out=dst, in_=src, mul=inv)
                 else:
                     nc.vector.tensor_scalar_mul(out=dst, in0=src, scalar1=inv)
             nc.sync.dma_start(out=ov[t][:, h * 2048 : (h + 1) * 2048], in_=ob[:])
 
         copy_x(0)
-        copy_x(1)
-        for n in range(NPOS):
+        for n in range(NV[0]):
             quant_x(0, n)
-        copy_g(0, 0)
-        copy_g(0, 1)
+        copy_x(1)
+        for n in range(NV[0], NPOS):
+            quant_x(0, n)
+        copy_g(0, 0, "V")
+        copy_g(0, 1, "S")
+        for n in range(3):
+            warm = psum.tile([P, CIN * BLK], F32, name="warm%d" % n, tag="ps")
+            nc.tensor.matmul(warm[:], lhsT=gg[0][:, 0, 0:P], rhs=gg[0][:, n, :], start=True, stop=True)
         for n in range(NPOS):
             quant_x(1, n)
-        copy_x(2)
         quant_g(0, 0)
         quant_g(0, 1)
+        early0 = [multiply(0, n, "a") for n in range(NPOS)]
+        copy_g(1, 0, "V")
+        copy_g(1, 1, "S")
+        copy_out(0, 0, early0)
+        quant_g(1, 0)
+        early1 = [multiply(1, n, "a") for n in range(4)]
+        copy_x(2)
+        quant_g(1, 1)
+        early1.extend([multiply(1, n, "a") for n in range(4, NPOS)])
+        copy_out(1, 0, early1)
         copy_x(3)
+        late0 = []
         for n in range(NPOS):
             quant_x(2, n)
             quant_x(3, n)
-        for t in range(n_tiles):
-            banks = multiply(t)
-            copy_out(t, 0, banks)
-            if t + 1 < n_tiles:
-                prepare_g(t + 1)
-            copy_out(t, 1, banks)
+            late0.append(multiply(0, n, "b"))
+        copy_out(0, 1, late0)
+        late1 = [multiply(1, n, "b") for n in range(NPOS)]
+        copy_out(1, 1, late1)
+        for t in (2, 3):
+            for h in range(2):
+                copy_g(t, h, "V")
+                quant_g(t, h)
+            banks = [multiply(t, n, "f") for n in range(NPOS)]
+            for h in range(2):
+                copy_out(t, h, banks, 4 if t == 3 else 0)

@@ -155,11 +155,10 @@ def tile_nonoverlappinglocallyconnected1d_kernel(tc, x, weight, grad_out, out):
         copy_g(1, 0, "V")
         copy_g(1, 1, "S")
         copy_out(0, 0, early0)
-        quant_g(1, 0)
-        early1 = [multiply(1, n, "a") for n in range(4)]
         copy_x(2)
+        quant_g(1, 0)
         quant_g(1, 1)
-        early1.extend([multiply(1, n, "a") for n in range(4, NPOS)])
+        early1 = [multiply(1, n, "a") for n in range(NPOS)]
         copy_out(1, 0, early1)
         copy_x(3)
         late0 = []
@@ -171,9 +170,10 @@ def tile_nonoverlappinglocallyconnected1d_kernel(tc, x, weight, grad_out, out):
         late1 = [multiply(1, n, "b") for n in range(NPOS)]
         copy_out(1, 1, late1)
         for t in (2, 3):
-            for h in range(2):
-                copy_g(t, h, "V")
-                quant_g(t, h)
+            copy_g(t, 0, "V")
+            copy_g(t, 1, "V")
+            quant_g(t, 0)
+            quant_g(t, 1)
             banks = [multiply(t, n, "f") for n in range(NPOS)]
             for h in range(2):
                 copy_out(t, h, banks, 4 if t == 3 else 0)

@@ -76,14 +76,11 @@ def tile_nonoverlappinglocallyconnected1d_kernel(tc, x, weight, grad_out, out):
             nv = NV[c]
             dst = grp.tile([P, NPOS, XC * 16], BF16, name="xg%d" % c, tag="grp", align_bytes=64)
             xg[c] = dst
-            nc.vector.tensor_copy(
-                out=dst[:].rearrange("p n (i k j) -> p i n j k", k=BLK, j=PACK)[:, :, 0:nv],
-                in_=xr[c][:].rearrange("p j (i n k) -> p i n j k", n=NPOS, k=BLK)[:, :, 0:nv],
-            )
-            for n in range(nv, NPOS):
-                nc.scalar.copy(
-                    out=dst[:, n, :].rearrange("p (i k j) -> p i j k", k=BLK, j=PACK),
-                    in_=xr[c][:].rearrange("p j (i n k) -> p n i j k", n=NPOS, k=BLK)[:, n],
+            for m in range(NPOS // 2):
+                copy = nc.vector.tensor_copy if 2 * m < nv else nc.scalar.copy
+                copy(
+                    out=dst[:, 2 * m : 2 * m + 2, :].rearrange("p n (i k j) -> p i j n k", k=BLK, j=PACK),
+                    in_=xr[c][:].rearrange("p j (i m n k) -> p m i j n k", m=NPOS // 2, n=2, k=BLK)[:, m],
                 )
 
         def quant_x(c, n):

@@ -21,7 +21,7 @@ NPOS = 8
 BLK = 4
 XC = 32
 HALF = CIN * BLK // 2
-NV = (4, 4, 6, 6)
+NV = (4, 4, 6, 8)
 LOADS = ("x0", "x1", "g0", "g1", "x2", "x3", "g23")
 
 

import math
from contextlib import ExitStack

import concourse.mybir as mybir

FLOPS = 2 * 8 * 512 * 512 * 512
BYTES = 2 * 512 * 128 * 32 + 2 * 512 * 512 * 8 + 4 * 512 * 128 * 32

BF16 = mybir.dt.bfloat16
F32 = mybir.dt.float32
U32 = mybir.dt.uint32
U8 = mybir.dt.uint8
E4M3X4 = mybir.dt.float8_e4m3fn_x4
E5M2X4 = mybir.dt.float8_e5m2_x4

P = 128
PACK = 4
CIN = 128
COUT = 512
NPOS = 8
BLK = 4
XC = 32
HALF = CIN * BLK // 2
NV = (4, 4, 6, 8)
LOADS = ("x0", "x1", "g0", "g1", "x2", "x3", "g23")


def tile_nonoverlappinglocallyconnected1d_kernel(tc, x, weight, grad_out, out):
    nc = tc.nc
    inv = 1.0 / math.sqrt(float(CIN))
    xv = x.rearrange("(p j) i d -> p j (i d)", j=PACK)
    gv = grad_out.rearrange("(p j) o n -> p j (o n)", j=PACK)
    ov = out.rearrange("(t o) i d -> t o (i d)", o=P)
    n_tiles = COUT // P
    gw = P * NPOS

    with ExitStack() as ctx:
        raw = ctx.enter_context(tc.tile_pool(name="raw", bufs=1))
        grp = ctx.enter_context(tc.tile_pool(name="grp", bufs=8))
        keep = ctx.enter_context(tc.tile_pool(name="keep", bufs=1))
        res = ctx.enter_context(tc.tile_pool(name="res", bufs=6))
        psum = ctx.enter_context(tc.psum_pool(name="psum", bufs=8))
        ctx.enter_context(tc.manual_schedule())

        xq = keep.tile([P, NPOS, CIN * BLK], U32, name="xq", align_bytes=64)
        xs = keep.tile([P, NPOS, CIN * BLK], U8, name="xs", align_bytes=64)
        gq = keep.tile([P, n_tiles, gw], U32, name="gq", align_bytes=64)
        gs = keep.tile([P, n_tiles, gw], U8, name="gs", align_bytes=64)

        xr = {}
        gr = {}

        def load_x(c):
            xr[c] = raw.tile([P, PACK, XC * 32], BF16, name="xr%d" % c)
            nc.sync.dma_start(out=xr[c][:], in_=xv[:, :, c * XC * 32 : (c + 1) * XC * 32])

        def load_g(t0, t1):
            buf = raw.tile([P, PACK, (t1 - t0) * gw], BF16, name="gr%d" % t0)
            nc.sync.dma_start(out=buf[:], in_=gv[:, :, t0 * gw : t1 * gw])
            for t in range(t0, t1):
                gr[t] = buf[:, :, (t - t0) * gw : (t - t0 + 1) * gw]

        for item in LOADS:
            if item[0] == "x":
                load_x(int(item[1:]))
            else:
                load_g(int(item[1]), int(item[-1]) + 1)

        nc.vector.memset(xq[:, :, HALF:], 0)
        nc.vector.memset(xs[:].bitcast(U32)[:, :, HALF // 4 :], 0)

        xg = {}
        gg = {}

        def copy_x(c):
            nv = NV[c]
            dst = grp.tile([P, NPOS, XC * 16], BF16, name="xg%d" % c, tag="grp", align_bytes=64)
            xg[c] = dst
            for m in range(NPOS // 2):
                copy = nc.vector.tensor_copy if 2 * m < nv else nc.scalar.copy
                copy(
                    out=dst[:, 2 * m : 2 * m + 2, :].rearrange("p n (i k j) -> p i j n k", k=BLK, j=PACK),
                    in_=xr[c][:].rearrange("p j (i m n k) -> p m i j n k", m=NPOS // 2, n=2, k=BLK)[:, m],
                )

        def quant_x(c, n):
            w0 = c * XC * BLK
            w1 = w0 + XC * BLK
            nc.vector.quantize_mx(
                out=xq[:, n, w0:w1].bitcast(E4M3X4),
                scales=xs[:, n, w0:w1],
                in_=xg[c][:, n, :],
            )

        def copy_g(t, h, engine):
            if h == 0:
                gg[t] = grp.tile([P, NPOS, P * PACK], BF16, name="gg%d" % t, tag="grp", align_bytes=64)
            dst = gg[t][:].rearrange("p (h l) (o j) -> p h o j l", l=4, j=PACK)[:, h]
            src = gr[t].rearrange("p j (o h l) -> p h o j l", h=2, l=4)[:, h]
            if engine == "S":
                nc.scalar.copy(out=dst, in_=src)
            else:
                nc.vector.tensor_copy(out=dst, in_=src)

        def quant_g(t, h):
            nc.vector.quantize_mx(
                out=gq[:, t, h * 512 : (h + 1) * 512].bitcast(E5M2X4),
                scales=gs[:, t, h * 512 : (h + 1) * 512],
                in_=gg[t][:, 4 * h : 4 * h + 4, :].rearrange("p n c -> p (n c)"),
            )

        def multiply(t, n, tag):
            ps = psum.tile([P, CIN * BLK], F32, name="ps%s%d_%d" % (tag, t, n), tag="ps")
            nc.tensor.matmul_mx(
                out=ps[:],
                lhsT=gq[:, t, n * P : (n + 1) * P].bitcast(E5M2X4),
                lhsT_scale=gs[:, t, n * P : (n + 1) * P],
                rhs=xq[:, n, :].bitcast(E4M3X4),
                rhs_scale=xs[:, n, :],
                start=True,
                stop=True,
            )
            return ps

        def copy_out(t, h, banks, nvec=0):
            ob = res.tile([P, 64 * 32], F32, name="ob%d_%d" % (t, h), tag="ob")
            for n in range(NPOS):
                dst = ob[:].rearrange("p (i n k) -> p i n k", n=NPOS, k=BLK)[:, :, n, :]
                src = banks[n][:, h * 256 : (h + 1) * 256].rearrange("p (i k) -> p i k", k=BLK)
                if n < NPOS - nvec:
                    nc.scalar.mul(out=dst, in_=src, mul=inv)
                else:
                    nc.vector.tensor_scalar_mul(out=dst, in0=src, scalar1=inv)
            nc.sync.dma_start(out=ov[t][:, h * 2048 : (h + 1) * 2048], in_=ob[:])

        copy_x(0)
        for n in range(NV[0]):
            quant_x(0, n)
        copy_x(1)
        for n in range(NV[0], NPOS):
            quant_x(0, n)
        copy_g(0, 0, "V")
        copy_g(0, 1, "S")
        for n in range(3):
            warm = psum.tile([P, CIN * BLK], F32, name="warm%d" % n, tag="ps")
            nc.tensor.matmul(warm[:], lhsT=gg[0][:, 0, 0:P], rhs=gg[0][:, n, :], start=True, stop=True)
        for n in range(NPOS):
            quant_x(1, n)
        quant_g(0, 0)
        quant_g(0, 1)
        early0 = [multiply(0, n, "a") for n in range(NPOS)]
        copy_g(1, 0, "V")
        copy_g(1, 1, "S")
        copy_out(0, 0, early0)
        copy_x(2)
        quant_g(1, 0)
        quant_g(1, 1)
        early1 = [multiply(1, n, "a") for n in range(NPOS)]
        copy_out(1, 0, early1)
        copy_x(3)
        late0 = []
        for n in range(NPOS):
            quant_x(2, n)
            quant_x(3, n)
            late0.append(multiply(0, n, "b"))
        copy_out(0, 1, late0)
        late1 = [multiply(1, n, "b") for n in range(NPOS)]
        copy_out(1, 1, late1)
        for t in (2, 3):
            copy_g(t, 0, "V")
            copy_g(t, 1, "V")
            quant_g(t, 0)
            quant_g(t, 1)
            banks = [multiply(t, n, "f") for n in range(NPOS)]
            for h in range(2):
                copy_out(t, h, banks, 4 if t == 3 else 0)
